import numpy as np
import ml_dtypes


def mxq(x, axis, fmt="e4m3"):
    dtype, down = {"e4m3": (ml_dtypes.float8_e4m3fn, 7), "e5m2": (ml_dtypes.float8_e5m2, 14)}[fmt]
    v = np.moveaxis(np.asarray(x, np.float32).astype(ml_dtypes.bfloat16).astype(np.float64), axis, -1)
    blocks = v.reshape(v.shape[:-1] + (-1, 32))
    amax = np.abs(blocks).max(-1, keepdims=True)
    byte = np.maximum(np.where(amax > 0, np.frexp(amax)[1] - 1 + 127, 0) - down, 1)
    scale = np.exp2(byte - 127.0)
    codes = (blocks / scale).astype(np.float32).astype(dtype).astype(np.float64)
    return np.moveaxis((codes * scale).reshape(v.shape), -1, axis)


WIDE = False


def mx_kscale(k):
    if not WIDE:
        return np.ones(k)
    levels = np.array([10, -10, 5, -5, 0])
    a = np.random.permutation(np.resize(levels, k // 512 * 4)).reshape(k // 512, 4)
    idx = np.arange(k)
    return np.exp2(a[idx // 512, idx % 128 // 32])


BF16 = ml_dtypes.bfloat16


def bf(x):
    return np.asarray(x, np.float32).astype(BF16)


def f64(x):
    return np.asarray(x).astype(np.float64)


B, S, H, I, G = 1, 128, 512, 512, 4
T = B * S


def grouped_linear(xf, w, b):
    g, dout, din = w.shape
    xg = xf.reshape(g, -1, din)
    y = (mxq(xg, 2, "e4m3") @ mxq(w, 2, "e4m3").transpose(0, 2, 1)) + b[:, None, :]
    return y.reshape(-1, dout)


def setup_inputs():
    s, t = mx_kscale(H), mx_kscale(I)
    return {"hf": bf(np.random.standard_normal((T, H)) * s),
            "g1_w": bf(np.random.standard_normal((G, I, H)) / np.sqrt(H) / s[None, None, :] * t[None, :, None]),
            "g1_b": bf(np.random.standard_normal((G, I)) * 0.3 * t[None, :]),
            "g2_w": bf(np.random.standard_normal((G, H, I)) / np.sqrt(I) / t[None, None, :]),
            "g2_b": bf(np.random.standard_normal((G, H)) * 0.3)}


def reference(hf, g1_w, g1_b, g2_w, g2_b):
    y = grouped_linear(f64(hf), f64(g1_w), f64(g1_b))
    return grouped_linear(y, f64(g2_w), f64(g2_b))

@@ -1,0 +1,167 @@
+from contextlib import ExitStack
+
+import concourse.mybir as mybir
+from concourse.masks import make_identity
+
+BF16 = mybir.dt.bfloat16
+F32 = mybir.dt.float32
+I32 = mybir.dt.int32
+U32 = mybir.dt.uint32
+U8 = mybir.dt.uint8
+FP8X4 = mybir.dt.float8_e4m3fn_x4
+
+P = 128
+PACK = 4
+K = P * PACK
+HALVES = 2
+GROUPS = 4
+TOKENS = 128
+GROUP_TOKENS = TOKENS // GROUPS
+FEATURES = 512
+BLOCKS = FEATURES // P
+BLOCKS_PER_BANK = 2
+LEAD = 2
+
+FLOPS = 2 * 2 * TOKENS * K * FEATURES
+
+
+def k_to_partitions(nc, banks, stage, identity, rows, blocks, tag):
+    words = rows.bitcast(F32)
+    grouped = stage.tile([P, blocks * P * PACK], BF16, align_bytes=64, tag=tag, name=tag)
+    grouped_words = grouped[:].bitcast(F32).rearrange("p (b r u) -> p b r u", r=P, u=HALVES)
+    for first in range(0, blocks, BLOCKS_PER_BANK):
+        count = min(BLOCKS_PER_BANK, blocks - first)
+        bank = banks.tile([P, count, HALVES, P], F32, tag="bank", name="bank")
+        for b in range(count):
+            for u in range(HALVES):
+                start = ((first + b) * HALVES + u) * P
+                nc.tensor.transpose(bank[:, b, u, :], words[:, start : start + P], identity)
+        nc.scalar.copy(
+            out=grouped_words[:, first : first + count],
+            in_=bank[:].rearrange("p b u r -> p b r u"),
+        )
+    return grouped
+
+
+def quantise(nc, keep, grouped, name):
+    columns = grouped.shape[1] // PACK
+    codes = keep.tile([P, columns], U32, align_bytes=64, name=name + "_codes")
+    scales = keep.tile([P, columns], U8, align_bytes=64, name=name + "_scales")
+    nc.vector.quantize_mx(out=codes[:].bitcast(FP8X4), scales=scales[:], in_=grouped[:])
+    return codes, scales
+
+
+def tile_dummytemodel_pa_s_kernel(tc, hf, g1_w, g1_b, g2_w, g2_b, out):
+    nc = tc.nc
+    with ExitStack() as ctx:
+        ctx.enter_context(tc.manual_schedule())
+        keep = ctx.enter_context(tc.tile_pool(name="keep", bufs=1))
+        stage = ctx.enter_context(tc.tile_pool(name="stage", bufs=3))
+        banks = ctx.enter_context(tc.psum_pool(name="banks", bufs=7))
+        out_bank = ctx.enter_context(tc.psum_pool(name="out_bank", bufs=1))
+
+        hf_rows = keep.tile([P, K], BF16)
+        nc.sync.dma_start(out=hf_rows[:], in_=hf)
+        w1_rows = []
+        w2_rows = []
+        for g in range(GROUPS):
+            rows = keep.tile([P, BLOCKS * K], BF16, name="w1_rows%d" % g)
+            nc.sync.dma_start(
+                out=rows[:].rearrange("r (u e k) -> r u e k", u=HALVES, e=2),
+                in_=g1_w[g].rearrange("(u r e) k -> r u e k", u=HALVES, e=2),
+            )
+            w1_rows.append(rows)
+        for g in range(GROUPS):
+            rows = keep.tile([P, BLOCKS * K], BF16, name="w2_rows%d" % g)
+            nc.sync.dma_start(out=rows[:], in_=g2_w[g].rearrange("(r j) k -> r (j k)", j=BLOCKS))
+            w2_rows.append(rows)
+        b2_rows = keep.tile([P, FEATURES], BF16)
+        for g in range(GROUPS):
+            nc.sync.dma_start(
+                out=b2_rows[g * GROUP_TOKENS : (g + 1) * GROUP_TOKENS, :],
+                in_=g2_b[g].partition_broadcast(GROUP_TOKENS),
+            )
+
+        identity = keep.tile([P, P], F32)
+        make_identity(nc, identity[:])
+        y_grouped = keep.tile([P, GROUPS, TOKENS, PACK], BF16, align_bytes=64)
+        nc.vector.memset(y_grouped[:].rearrange("p g t c -> p (g t c)").bitcast(I32), 0)
+        b1_rows = keep.tile([P, K // HALVES], BF16)
+        nc.vector.memset(b1_rows[:].bitcast(I32), 0)
+        nc.scalar.dma_start(
+            out=b1_rows[0 : GROUPS * HALVES, :],
+            in_=g1_b.rearrange("g (u c) -> (g u) c", u=HALVES),
+        )
+
+        x_grouped = k_to_partitions(nc, banks, stage, identity[:], hf_rows[:], 1, "x_grouped")
+        x_codes, x_scales = quantise(nc, keep, x_grouped, "x")
+
+        w1 = []
+        w2 = []
+        for g in range(GROUPS):
+            grouped = k_to_partitions(nc, banks, stage, identity[:], w1_rows[g][:], BLOCKS, "w_grouped")
+            w1.append(quantise(nc, keep, grouped, "w1_%d" % g))
+        for g in range(LEAD):
+            grouped = k_to_partitions(nc, banks, stage, identity[:], w2_rows[g][:], BLOCKS, "w_grouped")
+            w2.append(quantise(nc, keep, grouped, "w2_%d" % g))
+
+        b1_bank = banks.tile([P, P], F32, tag="bank", name="bank")
+        nc.tensor.transpose(b1_bank[:], b1_rows[:].bitcast(F32), identity[:])
+        b1_cols = keep.tile([P, GROUPS * PACK], F32)
+        nc.vector.tensor_copy(out=b1_cols[:], in_=b1_bank[:, 0 : GROUPS * HALVES].bitcast(BF16))
+
+        for g in range(GROUPS):
+            codes, scales = w1[g]
+            y_bank = banks.tile([P, PACK, TOKENS], F32, tag="bank", name="bank")
+            for t in range(PACK):
+                block = slice(t * P, (t + 1) * P)
+                nc.tensor.matmul_mx(
+                    out=y_bank[:, t, :],
+                    lhsT=codes[:, block].bitcast(FP8X4),
+                    lhsT_scale=scales[:, block],
+                    rhs=x_codes[:].bitcast(FP8X4),
+                    rhs_scale=x_scales[:],
+                    start=True,
+                    stop=True,
+                )
+            own = slice(g * GROUP_TOKENS, (g + 1) * GROUP_TOKENS)
+            nc.vector.tensor_tensor(
+                out=y_grouped[:, g, own, :],
+                in0=y_bank[:, :, own].rearrange("p c t -> p t c"),
+                in1=b1_cols[:, g * PACK : (g + 1) * PACK]
+                .unsqueeze(1)
+                .to_broadcast([P, GROUP_TOKENS, PACK]),
+                op=mybir.AluOpType.add,
+            )
+        y_codes = keep.tile([P, GROUPS, TOKENS], U32, align_bytes=64)
+        y_scales = keep.tile([P, GROUPS, TOKENS], U8, align_bytes=64)
+        nc.vector.quantize_mx(
+            out=y_codes[:].rearrange("p g t -> p (g t)").bitcast(FP8X4),
+            scales=y_scales[:].rearrange("p g t -> p (g t)"),
+            in_=y_grouped[:].rearrange("p g t c -> p (g t c)"),
+        )
+
+        for g in range(LEAD, GROUPS):
+            grouped = k_to_partitions(nc, banks, stage, identity[:], w2_rows[g][:], BLOCKS, "w_grouped")
+            w2.append(quantise(nc, keep, grouped, "w2_%d" % g))
+
+        acc = out_bank.tile([P, FEATURES], F32)
+        for g in range(GROUPS):
+            codes, scales = w2[g]
+            nc.tensor.matmul_mx(
+                out=acc[:],
+                lhsT=y_codes[:, g, :].bitcast(FP8X4),
+                lhsT_scale=y_scales[:, g, :],
+                rhs=codes[:].bitcast(FP8X4),
+                rhs_scale=scales[:],
+                start=(g == 0),
+                stop=(g == GROUPS - 1),
+            )
+        result = keep.tile([P, FEATURES], F32)
+        nc.vector.tensor_tensor(
+            out=result[:].rearrange("p (r j) -> p r j", j=BLOCKS),
+            in0=acc[:].rearrange("p (j r) -> p r j", j=BLOCKS),
+            in1=b2_rows[:].rearrange("p (r j) -> p r j", j=BLOCKS),
+            op=mybir.AluOpType.add,
+        )
+        nc.sync.dma_start(out=out, in_=result[:])

@@ -20,7 +20,7 @@ GROUP_TOKENS = TOKENS // GROUPS
 FEATURES = 512
 BLOCKS = FEATURES // P
 BLOCKS_PER_BANK = 2
-LEAD = 2
+LAG = 2
 
 FLOPS = 2 * 2 * TOKENS * K * FEATURES
 
@@ -96,22 +96,16 @@ def tile_dummytemodel_pa_s_kernel(tc, hf, g1_w, g1_b, g2_w, g2_b, out):
         x_grouped = k_to_partitions(nc, banks, stage, identity[:], hf_rows[:], 1, "x_grouped")
         x_codes, x_scales = quantise(nc, keep, x_grouped, "x")
 
-        w1 = []
-        w2 = []
-        for g in range(GROUPS):
-            grouped = k_to_partitions(nc, banks, stage, identity[:], w1_rows[g][:], BLOCKS, "w_grouped")
-            w1.append(quantise(nc, keep, grouped, "w1_%d" % g))
-        for g in range(LEAD):
-            grouped = k_to_partitions(nc, banks, stage, identity[:], w2_rows[g][:], BLOCKS, "w_grouped")
-            w2.append(quantise(nc, keep, grouped, "w2_%d" % g))
-
         b1_bank = banks.tile([P, P], F32, tag="bank", name="bank")
         nc.tensor.transpose(b1_bank[:], b1_rows[:].bitcast(F32), identity[:])
         b1_cols = keep.tile([P, GROUPS * PACK], F32)
         nc.vector.tensor_copy(out=b1_cols[:], in_=b1_bank[:, 0 : GROUPS * HALVES].bitcast(BF16))
 
-        for g in range(GROUPS):
-            codes, scales = w1[g]
+        y_codes = keep.tile([P, GROUPS, TOKENS], U32, align_bytes=64)
+        y_scales = keep.tile([P, GROUPS, TOKENS], U8, align_bytes=64)
+        acc = out_bank.tile([P, FEATURES], F32)
+
+        def layer_1(g, codes, scales):
             y_bank = banks.tile([P, PACK, TOKENS], F32, tag="bank", name="bank")
             for t in range(PACK):
                 block = slice(t * P, (t + 1) * P)
@@ -133,21 +127,13 @@ def tile_dummytemodel_pa_s_kernel(tc, hf, g1_w, g1_b, g2_w, g2_b, out):
                 .to_broadcast([P, GROUP_TOKENS, PACK]),
                 op=mybir.AluOpType.add,
             )
-        y_codes = keep.tile([P, GROUPS, TOKENS], U32, align_bytes=64)
-        y_scales = keep.tile([P, GROUPS, TOKENS], U8, align_bytes=64)
-        nc.vector.quantize_mx(
-            out=y_codes[:].rearrange("p g t -> p (g t)").bitcast(FP8X4),
-            scales=y_scales[:].rearrange("p g t -> p (g t)"),
-            in_=y_grouped[:].rearrange("p g t c -> p (g t c)"),
-        )
+            nc.vector.quantize_mx(
+                out=y_codes[:, g, :].bitcast(FP8X4),
+                scales=y_scales[:, g, :],
+                in_=y_grouped[:, g].rearrange("p t c -> p (t c)"),
+            )
 
-        for g in range(LEAD, GROUPS):
-            grouped = k_to_partitions(nc, banks, stage, identity[:], w2_rows[g][:], BLOCKS, "w_grouped")
-            w2.append(quantise(nc, keep, grouped, "w2_%d" % g))
-
-        acc = out_bank.tile([P, FEATURES], F32)
-        for g in range(GROUPS):
-            codes, scales = w2[g]
+        def layer_2(g, codes, scales):
             nc.tensor.matmul_mx(
                 out=acc[:],
                 lhsT=y_codes[:, g, :].bitcast(FP8X4),
@@ -157,6 +143,18 @@ def tile_dummytemodel_pa_s_kernel(tc, hf, g1_w, g1_b, g2_w, g2_b, out):
                 start=(g == 0),
                 stop=(g == GROUPS - 1),
             )
+
+        w_rows = w1_rows + w2_rows
+        w_quantised = []
+        for i in range(len(w_rows) + LAG):
+            if i < len(w_rows):
+                grouped = k_to_partitions(nc, banks, stage, identity[:], w_rows[i][:], BLOCKS, "w_grouped")
+                w_quantised.append(quantise(nc, keep, grouped, "w%d" % i))
+            if LAG <= i < LAG + GROUPS:
+                layer_1(i - LAG, *w_quantised[i - LAG])
+            if LAG + GROUPS <= i:
+                layer_2(i - LAG - GROUPS, *w_quantised[i - LAG])
+
         result = keep.tile([P, FEATURES], F32)
         nc.vector.tensor_tensor(
             out=result[:].rearrange("p (r j) -> p r j", j=BLOCKS),

@@ -21,6 +21,7 @@ FEATURES = 512
 BLOCKS = FEATURES // P
 BLOCKS_PER_BANK = 2
 LAG = 2
+WARM_PASSES = 6
 
 FLOPS = 2 * 2 * TOKENS * K * FEATURES
 
@@ -62,6 +63,12 @@ def tile_dummytemodel_pa_s_kernel(tc, hf, g1_w, g1_b, g2_w, g2_b, out):
 
         hf_rows = keep.tile([P, K], BF16)
         nc.sync.dma_start(out=hf_rows[:], in_=hf)
+        b1_rows = keep.tile([P, K // HALVES], BF16)
+        nc.vector.memset(b1_rows[:].bitcast(I32), 0)
+        nc.sync.dma_start(
+            out=b1_rows[0 : GROUPS * HALVES, :],
+            in_=g1_b.rearrange("g (u c) -> (g u) c", u=HALVES),
+        )
         w1_rows = []
         w2_rows = []
         for g in range(GROUPS):
@@ -84,14 +91,31 @@ def tile_dummytemodel_pa_s_kernel(tc, hf, g1_w, g1_b, g2_w, g2_b, out):
 
         identity = keep.tile([P, P], F32)
         make_identity(nc, identity[:])
+
         y_grouped = keep.tile([P, GROUPS, TOKENS, PACK], BF16, align_bytes=64)
+        y_codes = keep.tile([P, GROUPS, TOKENS], U32, align_bytes=64)
+        y_scales = keep.tile([P, GROUPS, TOKENS], U8, align_bytes=64)
         nc.vector.memset(y_grouped[:].rearrange("p g t c -> p (g t c)").bitcast(I32), 0)
-        b1_rows = keep.tile([P, K // HALVES], BF16)
-        nc.vector.memset(b1_rows[:].bitcast(I32), 0)
-        nc.scalar.dma_start(
-            out=b1_rows[0 : GROUPS * HALVES, :],
-            in_=g1_b.rearrange("g (u c) -> (g u) c", u=HALVES),
+        nc.vector.quantize_mx(
+            out=y_codes[:].rearrange("p g t -> p (g t)").bitcast(FP8X4),
+            scales=y_scales[:].rearrange("p g t -> p (g t)"),
+            in_=y_grouped[:].rearrange("p g t c -> p (g t c)"),
         )
+
+        def keep_warm(passes):
+            unread = banks.tile([P, FEATURES], F32, tag="bank", name="bank")
+            for n in range(passes):
+                nc.tensor.matmul_mx(
+                    out=unread[:],
+                    lhsT=y_codes[:, 0, :].bitcast(FP8X4),
+                    lhsT_scale=y_scales[:, 0, :],
+                    rhs=y_codes[:].rearrange("p g t -> p (g t)").bitcast(FP8X4),
+                    rhs_scale=y_scales[:].rearrange("p g t -> p (g t)"),
+                    start=True,
+                    stop=True,
+                )
+
+        keep_warm(WARM_PASSES)
 
         x_grouped = k_to_partitions(nc, banks, stage, identity[:], hf_rows[:], 1, "x_grouped")
         x_codes, x_scales = quantise(nc, keep, x_grouped, "x")
@@ -101,8 +125,6 @@ def tile_dummytemodel_pa_s_kernel(tc, hf, g1_w, g1_b, g2_w, g2_b, out):
         b1_cols = keep.tile([P, GROUPS * PACK], F32)
         nc.vector.tensor_copy(out=b1_cols[:], in_=b1_bank[:, 0 : GROUPS * HALVES].bitcast(BF16))
 
-        y_codes = keep.tile([P, GROUPS, TOKENS], U32, align_bytes=64)
-        y_scales = keep.tile([P, GROUPS, TOKENS], U8, align_bytes=64)
         acc = out_bank.tile([P, FEATURES], F32)
 
         def layer_1(g, codes, scales):
@@ -150,9 +172,11 @@ def tile_dummytemodel_pa_s_kernel(tc, hf, g1_w, g1_b, g2_w, g2_b, out):
             if i < len(w_rows):
                 grouped = k_to_partitions(nc, banks, stage, identity[:], w_rows[i][:], BLOCKS, "w_grouped")
                 w_quantised.append(quantise(nc, keep, grouped, "w%d" % i))
-            if LAG <= i < LAG + GROUPS:
+            if i < LAG:
+                keep_warm(1)
+            elif i < LAG + GROUPS:
                 layer_1(i - LAG, *w_quantised[i - LAG])
-            if LAG + GROUPS <= i:
+            else:
                 layer_2(i - LAG - GROUPS, *w_quantised[i - LAG])
 
         result = keep.tile([P, FEATURES], F32)

from contextlib import ExitStack

import concourse.mybir as mybir
from concourse.masks import make_identity

BF16 = mybir.dt.bfloat16
F32 = mybir.dt.float32
I32 = mybir.dt.int32
U32 = mybir.dt.uint32
U8 = mybir.dt.uint8
FP8X4 = mybir.dt.float8_e4m3fn_x4

P = 128
PACK = 4
K = P * PACK
HALVES = 2
GROUPS = 4
TOKENS = 128
GROUP_TOKENS = TOKENS // GROUPS
FEATURES = 512
BLOCKS = FEATURES // P
BLOCKS_PER_BANK = 2
LAG = 2
WARM_PASSES = 6

FLOPS = 2 * 2 * TOKENS * K * FEATURES


def k_to_partitions(nc, banks, stage, identity, rows, blocks, tag):
    words = rows.bitcast(F32)
    grouped = stage.tile([P, blocks * P * PACK], BF16, align_bytes=64, tag=tag, name=tag)
    grouped_words = grouped[:].bitcast(F32).rearrange("p (b r u) -> p b r u", r=P, u=HALVES)
    for first in range(0, blocks, BLOCKS_PER_BANK):
        count = min(BLOCKS_PER_BANK, blocks - first)
        bank = banks.tile([P, count, HALVES, P], F32, tag="bank", name="bank")
        for b in range(count):
            for u in range(HALVES):
                start = ((first + b) * HALVES + u) * P
                nc.tensor.transpose(bank[:, b, u, :], words[:, start : start + P], identity)
        nc.scalar.copy(
            out=grouped_words[:, first : first + count],
            in_=bank[:].rearrange("p b u r -> p b r u"),
        )
    return grouped


def quantise(nc, keep, grouped, name):
    columns = grouped.shape[1] // PACK
    codes = keep.tile([P, columns], U32, align_bytes=64, name=name + "_codes")
    scales = keep.tile([P, columns], U8, align_bytes=64, name=name + "_scales")
    nc.vector.quantize_mx(out=codes[:].bitcast(FP8X4), scales=scales[:], in_=grouped[:])
    return codes, scales


def tile_dummytemodel_pa_s_kernel(tc, hf, g1_w, g1_b, g2_w, g2_b, out):
    nc = tc.nc
    with ExitStack() as ctx:
        ctx.enter_context(tc.manual_schedule())
        keep = ctx.enter_context(tc.tile_pool(name="keep", bufs=1))
        stage = ctx.enter_context(tc.tile_pool(name="stage", bufs=3))
        banks = ctx.enter_context(tc.psum_pool(name="banks", bufs=7))
        out_bank = ctx.enter_context(tc.psum_pool(name="out_bank", bufs=1))

        hf_rows = keep.tile([P, K], BF16)
        nc.sync.dma_start(out=hf_rows[:], in_=hf)
        b1_rows = keep.tile([P, K // HALVES], BF16)
        nc.vector.memset(b1_rows[:].bitcast(I32), 0)
        nc.sync.dma_start(
            out=b1_rows[0 : GROUPS * HALVES, :],
            in_=g1_b.rearrange("g (u c) -> (g u) c", u=HALVES),
        )
        w1_rows = []
        w2_rows = []
        for g in range(GROUPS):
            rows = keep.tile([P, BLOCKS * K], BF16, name="w1_rows%d" % g)
            nc.sync.dma_start(
                out=rows[:].rearrange("r (u e k) -> r u e k", u=HALVES, e=2),
                in_=g1_w[g].rearrange("(u r e) k -> r u e k", u=HALVES, e=2),
            )
            w1_rows.append(rows)
        for g in range(GROUPS):
            rows = keep.tile([P, BLOCKS * K], BF16, name="w2_rows%d" % g)
            nc.sync.dma_start(out=rows[:], in_=g2_w[g].rearrange("(r j) k -> r (j k)", j=BLOCKS))
            w2_rows.append(rows)
        b2_rows = keep.tile([P, FEATURES], BF16)
        for g in range(GROUPS):
            nc.sync.dma_start(
                out=b2_rows[g * GROUP_TOKENS : (g + 1) * GROUP_TOKENS, :],
                in_=g2_b[g].partition_broadcast(GROUP_TOKENS),
            )

        identity = keep.tile([P, P], F32)
        make_identity(nc, identity[:])

        y_grouped = keep.tile([P, GROUPS, TOKENS, PACK], BF16, align_bytes=64)
        y_codes = keep.tile([P, GROUPS, TOKENS], U32, align_bytes=64)
        y_scales = keep.tile([P, GROUPS, TOKENS], U8, align_bytes=64)
        nc.vector.memset(y_grouped[:].rearrange("p g t c -> p (g t c)").bitcast(I32), 0)
        nc.vector.quantize_mx(
            out=y_codes[:].rearrange("p g t -> p (g t)").bitcast(FP8X4),
            scales=y_scales[:].rearrange("p g t -> p (g t)"),
            in_=y_grouped[:].rearrange("p g t c -> p (g t c)"),
        )

        def keep_warm(passes):
            unread = banks.tile([P, FEATURES], F32, tag="bank", name="bank")
            for n in range(passes):
                nc.tensor.matmul_mx(
                    out=unread[:],
                    lhsT=y_codes[:, 0, :].bitcast(FP8X4),
                    lhsT_scale=y_scales[:, 0, :],
                    rhs=y_codes[:].rearrange("p g t -> p (g t)").bitcast(FP8X4),
                    rhs_scale=y_scales[:].rearrange("p g t -> p (g t)"),
                    start=True,
                    stop=True,
                )

        keep_warm(WARM_PASSES)

        x_grouped = k_to_partitions(nc, banks, stage, identity[:], hf_rows[:], 1, "x_grouped")
        x_codes, x_scales = quantise(nc, keep, x_grouped, "x")

        b1_bank = banks.tile([P, P], F32, tag="bank", name="bank")
        nc.tensor.transpose(b1_bank[:], b1_rows[:].bitcast(F32), identity[:])
        b1_cols = keep.tile([P, GROUPS * PACK], F32)
        nc.vector.tensor_copy(out=b1_cols[:], in_=b1_bank[:, 0 : GROUPS * HALVES].bitcast(BF16))

        acc = out_bank.tile([P, FEATURES], F32)

        def layer_1(g, codes, scales):
            y_bank = banks.tile([P, PACK, TOKENS], F32, tag="bank", name="bank")
            for t in range(PACK):
                block = slice(t * P, (t + 1) * P)
                nc.tensor.matmul_mx(
                    out=y_bank[:, t, :],
                    lhsT=codes[:, block].bitcast(FP8X4),
                    lhsT_scale=scales[:, block],
                    rhs=x_codes[:].bitcast(FP8X4),
                    rhs_scale=x_scales[:],
                    start=True,
                    stop=True,
                )
            own = slice(g * GROUP_TOKENS, (g + 1) * GROUP_TOKENS)
            nc.vector.tensor_tensor(
                out=y_grouped[:, g, own, :],
                in0=y_bank[:, :, own].rearrange("p c t -> p t c"),
                in1=b1_cols[:, g * PACK : (g + 1) * PACK]
                .unsqueeze(1)
                .to_broadcast([P, GROUP_TOKENS, PACK]),
                op=mybir.AluOpType.add,
            )
            nc.vector.quantize_mx(
                out=y_codes[:, g, :].bitcast(FP8X4),
                scales=y_scales[:, g, :],
                in_=y_grouped[:, g].rearrange("p t c -> p (t c)"),
            )

        def layer_2(g, codes, scales):
            nc.tensor.matmul_mx(
                out=acc[:],
                lhsT=y_codes[:, g, :].bitcast(FP8X4),
                lhsT_scale=y_scales[:, g, :],
                rhs=codes[:].bitcast(FP8X4),
                rhs_scale=scales[:],
                start=(g == 0),
                stop=(g == GROUPS - 1),
            )

        w_rows = w1_rows + w2_rows
        w_quantised = []
        for i in range(len(w_rows) + LAG):
            if i < len(w_rows):
                grouped = k_to_partitions(nc, banks, stage, identity[:], w_rows[i][:], BLOCKS, "w_grouped")
                w_quantised.append(quantise(nc, keep, grouped, "w%d" % i))
            if i < LAG:
                keep_warm(1)
            elif i < LAG + GROUPS:
                layer_1(i - LAG, *w_quantised[i - LAG])
            else:
                layer_2(i - LAG - GROUPS, *w_quantised[i - LAG])

        result = keep.tile([P, FEATURES], F32)
        nc.vector.tensor_tensor(
            out=result[:].rearrange("p (r j) -> p r j", j=BLOCKS),
            in0=acc[:].rearrange("p (j r) -> p r j", j=BLOCKS),
            in1=b2_rows[:].rearrange("p (r j) -> p r j", j=BLOCKS),
            op=mybir.AluOpType.add,
        )
        nc.sync.dma_start(out=out, in_=result[:])
